import numpy as np
import ml_dtypes


def mxq(x, axis, fmt="e4m3"):
    dtype, down = {"e4m3": (ml_dtypes.float8_e4m3fn, 7), "e5m2": (ml_dtypes.float8_e5m2, 14)}[fmt]
    v = np.moveaxis(np.asarray(x, np.float32).astype(ml_dtypes.bfloat16).astype(np.float64), axis, -1)
    blocks = v.reshape(v.shape[:-1] + (-1, 32))
    amax = np.abs(blocks).max(-1, keepdims=True)
    byte = np.maximum(np.where(amax > 0, np.frexp(amax)[1] - 1 + 127, 0) - down, 1)
    scale = np.exp2(byte - 127.0)
    codes = (blocks / scale).astype(np.float32).astype(dtype).astype(np.float64)
    return np.moveaxis((codes * scale).reshape(v.shape), -1, axis)


WIDE = False


def mx_kscale(k):
    if not WIDE:
        return np.ones(k)
    levels = np.array([10, -10, 5, -5, 0])
    a = np.random.permutation(np.resize(levels, k // 512 * 4)).reshape(k // 512, 4)
    idx = np.arange(k)
    return np.exp2(a[idx // 512, idx % 128 // 32])


BF16 = ml_dtypes.bfloat16


def bf(x):
    return np.asarray(x, np.float32).astype(BF16)


def f64(x):
    return np.asarray(x).astype(np.float64)


N, K, F, H, O, Q, GS, SO = 128, 16, 512, 1024, 1024, 1024, 3, 2


def setup_inputs():
    s, t = mx_kscale(F), mx_kscale(H)
    return {"x": bf(np.random.standard_normal((N, F)) * s),
            "contexts": bf(np.random.standard_normal((N, K, F)) * s),
            "attn": bf(np.random.random((N, K))),
            "Wn": bf(np.random.standard_normal((H, F)) * 0.5 / np.sqrt(F) / s * t[:, None]),
            "bn": bf(np.random.standard_normal(H) * 0.1 * t),
            "Wc": bf(np.random.standard_normal((H, F)) * 1.5 / np.sqrt(F) / s * t[:, None]),
            "bc": bf(np.random.standard_normal(H) * 0.1 * t),
            "Wu": bf(np.random.standard_normal((O, H)) * 1.5 / np.sqrt(H) / t),
            "bu": bf(np.random.standard_normal(O) * 0.1)}


def reference(x, contexts, attn, Wn, bn, Wc, bc, Wu, bu):
    xt = (mxq(f64(x), 1, "e4m3") @ mxq(f64(Wn).T, 0, "e4m3")) + f64(bn)
    ct = (mxq(f64(contexts).reshape(N * K, F), 1, "e4m3") @ mxq(f64(Wc).T, 0, "e4m3")).reshape(N, K, H) + f64(bc)
    ca = (ct * f64(attn)[..., None]).mean(axis=1)
    return (mxq(xt + ca, 1, "e4m3") @ mxq(f64(Wu).T, 0, "e4m3")) + f64(bu)

@@ -1,0 +1,247 @@
+from contextlib import ExitStack
+
+import concourse.mybir as mybir
+from concourse.masks import make_identity
+
+F32 = mybir.dt.float32
+BF16 = mybir.dt.bfloat16
+U32 = mybir.dt.uint32
+U8 = mybir.dt.uint8
+FP8X4 = mybir.dt.float8_e4m3fn_x4
+MULT = mybir.AluOpType.mult
+ADD = mybir.AluOpType.add
+COPY = mybir.ActivationFunctionType.Copy
+
+P = 128
+PACK = 4
+K_PASS = P * PACK
+BANK = 512
+
+NODES = 128
+CONTEXTS = 16
+F_IN = 512
+HIDDEN = 1024
+F_OUT = 1024
+HALVES = HIDDEN // K_PASS
+
+GROUP = 4
+BLOCKS_PER_BANK = 2
+PREPARED_PER_ROUND = 2
+
+FLOPS = 2 * (NODES * F_IN * HIDDEN + NODES * CONTEXTS * F_IN * HIDDEN + NODES * HIDDEN * F_OUT)
+
+
+def tile_nodeembeddinglayer_pa_kernel(tc, x, contexts, attn, Wn, bn, Wc, bc, Wu, bu, out):
+    nc = tc.nc
+    with ExitStack() as stack:
+        stack.enter_context(tc.manual_schedule())
+        keep = stack.enter_context(tc.tile_pool(name="keep", bufs=1))
+        turned_pool = stack.enter_context(tc.psum_pool(name="turned_pool", bufs=4))
+        product_pool = stack.enter_context(tc.psum_pool(name="product_pool", bufs=4))
+
+        attn_raw = keep.tile([P, CONTEXTS], BF16, name="attn_raw")
+        nc.scalar.dma_start(out=attn_raw[:], in_=attn)
+        bias_rows = keep.tile([P, HIDDEN], BF16, name="bias_rows")
+        nc.vector.memset(bias_rows[:], 0.0)
+        nc.scalar.dma_start(out=bias_rows[0:CONTEXTS, :], in_=bc.partition_broadcast(CONTEXTS))
+        nc.scalar.dma_start(out=bias_rows[CONTEXTS : CONTEXTS + 1, :], in_=bn.unsqueeze(0))
+
+        wc_raw = keep.tile([P, HALVES * GROUP * F_IN], BF16, name="wc_raw")
+        wn_raw = keep.tile([P, HALVES * GROUP * F_IN], BF16, name="wn_raw")
+        ctx_raw = keep.tile([P, CONTEXTS * F_IN], BF16, name="ctx_raw")
+        x_raw = keep.tile([P, F_IN], BF16, name="x_raw")
+        wu_raw = keep.tile([P, (F_OUT // P) * HIDDEN], BF16, name="wu_raw")
+        bu_rows = keep.tile([P, F_OUT], BF16, name="bu_rows")
+
+        def load_hidden_rows(raw, weight, half):
+            nc.sync.dma_start(
+                out=raw[:, half * GROUP * F_IN : (half + 1) * GROUP * F_IN].rearrange("p (u ef) -> p u ef", u=2),
+                in_=weight.rearrange("(g u p e) f -> g p u (e f)", g=HALVES, u=2, p=P, e=2)[half],
+            )
+
+        def load_contexts(group):
+            columns = slice(group * GROUP * F_IN, (group + 1) * GROUP * F_IN)
+            nc.sync.dma_start(out=ctx_raw[:, columns], in_=contexts.rearrange("n k f -> n (k f)")[:, columns])
+
+        def load_output_rows(side):
+            nc.sync.dma_start(
+                out=wu_raw[:, side * GROUP * HIDDEN : (side + 1) * GROUP * HIDDEN].rearrange(
+                    "p (b h) -> p b h", b=GROUP
+                ),
+                in_=Wu.rearrange("(b p) h -> p b h", p=P)[:, side * GROUP : (side + 1) * GROUP, :],
+            )
+
+        load_hidden_rows(wc_raw, Wc, 0)
+        for group in range(CONTEXTS // GROUP):
+            load_contexts(group)
+        nc.sync.dma_start(out=x_raw[:], in_=x)
+        load_hidden_rows(wn_raw, Wn, 0)
+        load_hidden_rows(wc_raw, Wc, 1)
+        load_hidden_rows(wn_raw, Wn, 1)
+        load_output_rows(0)
+        load_output_rows(1)
+        nc.sync.dma_start(out=bu_rows[:], in_=bu.partition_broadcast(P))
+
+        identity_words = keep.tile([P, P], F32, name="identity_words")
+        make_identity(nc, identity_words[:])
+        identity_values = keep.tile([P, P], BF16, name="identity_values")
+        make_identity(nc, identity_values[:])
+
+        def new_operand(name, source):
+            columns = source.shape[1] * P
+            return {
+                "source": source,
+                "grouped": keep.tile([P, columns * PACK], BF16, name=name + "_grouped", align_bytes=64),
+                "codes": keep.tile([P, columns], U32, name=name + "_codes", align_bytes=64),
+                "scales": keep.tile([P, columns], U8, name=name + "_scales", align_bytes=64),
+            }
+
+        def words(raw, blocks):
+            return raw[:].bitcast(F32).rearrange("p (b w) -> p b w", b=blocks)
+
+        def turn(operand, copies):
+            source = operand["source"]
+            as_words = source.dtype == F32
+            identity = identity_words if as_words else identity_values
+            grouped = operand["grouped"][:].bitcast(F32) if as_words else operand["grouped"][:]
+            blocks = source.shape[1]
+            planes = source.shape[2] // P
+            in_bank = min(blocks, BLOCKS_PER_BANK)
+            for bank in range(blocks // in_bank):
+                turned = turned_pool.tile([P, in_bank, planes, P], source.dtype, tag="turned")
+                for i in range(in_bank):
+                    for plane in range(planes):
+                        nc.tensor.transpose(
+                            turned[:, i, plane, :],
+                            source[:, bank * in_bank + i, plane * P : (plane + 1) * P],
+                            identity[:],
+                        )
+                width = in_bank * P * planes
+                copies[bank](
+                    out=grouped[:, bank * width : (bank + 1) * width].rearrange(
+                        "p (i r u) -> p i r u", i=in_bank, u=planes
+                    ),
+                    in_=turned[:].rearrange("p i u r -> p i r u"),
+                )
+
+        def quantise(operand):
+            nc.vector.quantize_mx(
+                out=operand["codes"][:].bitcast(FP8X4), scales=operand["scales"][:], in_=operand["grouped"][:]
+            )
+
+        def mx_pass(acc, stationary, block, moving, start, stop):
+            columns = slice(block * P, (block + 1) * P)
+            nc.tensor.matmul_mx(
+                out=acc[:],
+                lhsT=stationary["codes"][:, columns].bitcast(FP8X4),
+                lhsT_scale=stationary["scales"][:, columns],
+                rhs=moving["codes"][:].bitcast(FP8X4),
+                rhs_scale=moving["scales"][:],
+                start=start,
+                stop=stop,
+            )
+
+        by_scalar = (nc.scalar.copy, nc.scalar.copy)
+        shared = (nc.scalar.copy, nc.vector.tensor_copy)
+
+        ctx_words = words(ctx_raw, CONTEXTS)
+        wc_words = words(wc_raw, HALVES * GROUP)
+        wn_words = words(wn_raw, HALVES * GROUP)
+        wu_words = words(wu_raw, F_OUT // P)
+        h_values = [keep.tile([P, K_PASS], BF16, name="h_values%d" % half) for half in range(HALVES)]
+
+        ctx_ops = [
+            new_operand("ctx%d" % g, ctx_words[:, g * GROUP : (g + 1) * GROUP, :]) for g in range(CONTEXTS // GROUP)
+        ]
+        x_op = new_operand("x", words(x_raw, 1))
+        wc_ops = [new_operand("wc%d" % g, wc_words[:, g * GROUP : (g + 1) * GROUP, :]) for g in range(HALVES)]
+        wn_ops = [new_operand("wn%d" % g, wn_words[:, g * GROUP : (g + 1) * GROUP, :]) for g in range(HALVES)]
+        h_ops = [
+            new_operand("h%d" % g, h_values[g][:].rearrange("p (b v) -> p b v", b=1)) for g in range(HALVES)
+        ]
+        wu_ops = [
+            [
+                new_operand(
+                    "wu%d%d" % (g, side),
+                    wu_words[:, side * GROUP : (side + 1) * GROUP, g * K_PASS // 2 : (g + 1) * K_PASS // 2],
+                )
+                for side in range(F_OUT // BANK)
+            ]
+            for g in range(HALVES)
+        ]
+
+        mean_weights = keep.tile([P, CONTEXTS], F32, name="mean_weights")
+        nc.scalar.activation(out=mean_weights[:], in_=attn_raw[:], func=COPY, scale=1.0 / CONTEXTS)
+        bias_weights = keep.tile([P, P], BF16, name="bias_weights")
+        nc.vector.memset(bias_weights[:], 0.0)
+        nc.vector.memset(bias_weights[:, CONTEXTS : CONTEXTS + 1], 1.0)
+
+        turn(wc_ops[0], shared)
+        turn(ctx_ops[0], shared)
+        quantise(wc_ops[0])
+        quantise(ctx_ops[0])
+        turn(ctx_ops[1], by_scalar)
+
+        nc.vector.tensor_copy(out=bias_weights[:, 0:CONTEXTS], in_=mean_weights[:])
+        bias_turned = turned_pool.tile([P, P], BF16, tag="turned")
+        nc.tensor.transpose(bias_turned[:], bias_weights[:], identity_values[:])
+        bias_weights_t = keep.tile([P, P], BF16, name="bias_weights_t")
+        nc.scalar.copy(out=bias_weights_t[:], in_=bias_turned[:])
+
+        turned_last_round = [ctx_ops[1]]
+        waiting = [
+            ctx_ops[2], ctx_ops[3], x_op, wn_ops[0], wc_ops[1], wn_ops[1],
+            wu_ops[0][0], wu_ops[1][0], h_ops[0], wu_ops[0][1], wu_ops[1][1],
+        ]
+        for half in range(HALVES):
+            sums = [keep.tile([P, BANK], F32, name="sum%d_%d" % (half, c)) for c in range(2)]
+            for group in range(CONTEXTS // GROUP):
+                products = []
+                for i in range(GROUP):
+                    product = product_pool.tile([P, BANK], F32, tag="product")
+                    mx_pass(product, ctx_ops[group], i, wc_ops[half], True, True)
+                    products.append(product)
+                for operand in turned_last_round:
+                    quantise(operand)
+                for i in range(GROUP):
+                    k = group * GROUP + i
+                    weight = mean_weights[:, k : k + 1]
+                    if k < 2:
+                        nc.scalar.activation(out=sums[k][:], in_=products[i][:], func=COPY, scale=weight)
+                    else:
+                        nc.vector.scalar_tensor_tensor(
+                            out=sums[k % 2][:], in0=products[i][:], scalar=weight, in1=sums[k % 2][:],
+                            op0=MULT, op1=ADD,
+                        )
+                turned_last_round = waiting[:PREPARED_PER_ROUND]
+                waiting = waiting[PREPARED_PER_ROUND:]
+                for operand in turned_last_round:
+                    turn(operand, by_scalar)
+            xt = product_pool.tile([P, BANK], F32, tag="product")
+            mx_pass(xt, x_op, 0, wn_ops[half], True, True)
+            biases = product_pool.tile([P, BANK], F32, tag="product")
+            nc.tensor.matmul(
+                out=biases[:], lhsT=bias_weights_t[:], rhs=bias_rows[:, half * BANK : (half + 1) * BANK],
+                start=True, stop=True,
+            )
+            nc.vector.tensor_add(out=sums[0][:], in0=xt[:], in1=sums[0][:])
+            in_h_order = sums[1][:].rearrange("n (u e p) -> n u e p", u=2, e=2)
+            nc.vector.tensor_tensor(
+                out=in_h_order, in0=biases[:].rearrange("n (u p e) -> n u e p", u=2, e=2), in1=in_h_order, op=ADD
+            )
+            nc.vector.tensor_add(out=h_values[half][:], in0=sums[0][:], in1=sums[1][:])
+
+        sides = range(F_OUT // BANK)
+        out_sums = []
+        for side in sides:
+            out_sum = product_pool.tile([P, BANK], F32, tag="product")
+            mx_pass(out_sum, h_ops[0], 0, wu_ops[0][side], True, False)
+            out_sums.append(out_sum)
+        turn(h_ops[1], by_scalar)
+        quantise(h_ops[1])
+        result = keep.tile([P, F_OUT], F32, name="result")
+        for side in sides:
+            columns = slice(side * BANK, (side + 1) * BANK)
+            mx_pass(out_sums[side], h_ops[1], 0, wu_ops[1][side], False, True)
+            nc.vector.tensor_add(out=result[:, columns], in0=out_sums[side][:], in1=bu_rows[:, columns])
+            nc.sync.dma_start(out=out[:, columns], in_=result[:, columns])

@@ -23,9 +23,10 @@ F_IN = 512
 HIDDEN = 1024
 F_OUT = 1024
 HALVES = HIDDEN // K_PASS
+SIDES = F_OUT // BANK
 
 GROUP = 4
-BLOCKS_PER_BANK = 2
+PAIR = 2
 PREPARED_PER_ROUND = 2
 
 FLOPS = 2 * (NODES * F_IN * HIDDEN + NODES * CONTEXTS * F_IN * HIDDEN + NODES * HIDDEN * F_OUT)
@@ -50,36 +51,38 @@ def tile_nodeembeddinglayer_pa_kernel(tc, x, contexts, attn, Wn, bn, Wc, bc, Wu,
         wn_raw = keep.tile([P, HALVES * GROUP * F_IN], BF16, name="wn_raw")
         ctx_raw = keep.tile([P, CONTEXTS * F_IN], BF16, name="ctx_raw")
         x_raw = keep.tile([P, F_IN], BF16, name="x_raw")
-        wu_raw = keep.tile([P, (F_OUT // P) * HIDDEN], BF16, name="wu_raw")
+        wu_raw = keep.tile([P, SIDES * GROUP * HIDDEN], BF16, name="wu_raw")
         bu_rows = keep.tile([P, F_OUT], BF16, name="bu_rows")
 
         def load_hidden_rows(raw, weight, half):
-            nc.sync.dma_start(
-                out=raw[:, half * GROUP * F_IN : (half + 1) * GROUP * F_IN].rearrange("p (u ef) -> p u ef", u=2),
-                in_=weight.rearrange("(g u p e) f -> g p u (e f)", g=HALVES, u=2, p=P, e=2)[half],
-            )
+            for u in range(2):
+                pair = half * 2 + u
+                nc.sync.dma_start(
+                    out=raw[:, pair * PAIR * F_IN : (pair + 1) * PAIR * F_IN],
+                    in_=weight.rearrange("(g p e) f -> g p (e f)", g=HALVES * 2, p=P, e=PAIR)[pair],
+                )
 
-        def load_contexts(group):
-            columns = slice(group * GROUP * F_IN, (group + 1) * GROUP * F_IN)
+        def load_contexts(pair):
+            columns = slice(pair * PAIR * F_IN, (pair + 1) * PAIR * F_IN)
             nc.sync.dma_start(out=ctx_raw[:, columns], in_=contexts.rearrange("n k f -> n (k f)")[:, columns])
 
-        def load_output_rows(side):
+        def load_output_rows(pair):
             nc.sync.dma_start(
-                out=wu_raw[:, side * GROUP * HIDDEN : (side + 1) * GROUP * HIDDEN].rearrange(
-                    "p (b h) -> p b h", b=GROUP
+                out=wu_raw[:, pair * PAIR * HIDDEN : (pair + 1) * PAIR * HIDDEN].rearrange(
+                    "p (b h) -> p b h", b=PAIR
                 ),
-                in_=Wu.rearrange("(b p) h -> p b h", p=P)[:, side * GROUP : (side + 1) * GROUP, :],
+                in_=Wu.rearrange("(b p) h -> p b h", p=P)[:, pair * PAIR : (pair + 1) * PAIR, :],
             )
 
         load_hidden_rows(wc_raw, Wc, 0)
-        for group in range(CONTEXTS // GROUP):
-            load_contexts(group)
+        for pair in range(CONTEXTS // PAIR):
+            load_contexts(pair)
         nc.sync.dma_start(out=x_raw[:], in_=x)
         load_hidden_rows(wn_raw, Wn, 0)
         load_hidden_rows(wc_raw, Wc, 1)
         load_hidden_rows(wn_raw, Wn, 1)
-        load_output_rows(0)
-        load_output_rows(1)
+        for pair in range(SIDES * GROUP // PAIR):
+            load_output_rows(pair)
         nc.sync.dma_start(out=bu_rows[:], in_=bu.partition_broadcast(P))
 
         identity_words = keep.tile([P, P], F32, name="identity_words")
@@ -96,37 +99,41 @@ def tile_nodeembeddinglayer_pa_kernel(tc, x, contexts, attn, Wn, bn, Wc, bc, Wu,
                 "scales": keep.tile([P, columns], U8, name=name + "_scales", align_bytes=64),
             }
 
+        def pairs_of(operand):
+            blocks = operand["source"].shape[1]
+            step = min(blocks, PAIR)
+            return [(operand, first, step) for first in range(0, blocks, step)]
+
         def words(raw, blocks):
             return raw[:].bitcast(F32).rearrange("p (b w) -> p b w", b=blocks)
 
-        def turn(operand, copies):
+        def turn(piece, copy_out):
+            operand, first, count = piece
             source = operand["source"]
             as_words = source.dtype == F32
             identity = identity_words if as_words else identity_values
             grouped = operand["grouped"][:].bitcast(F32) if as_words else operand["grouped"][:]
-            blocks = source.shape[1]
             planes = source.shape[2] // P
-            in_bank = min(blocks, BLOCKS_PER_BANK)
-            for bank in range(blocks // in_bank):
-                turned = turned_pool.tile([P, in_bank, planes, P], source.dtype, tag="turned")
-                for i in range(in_bank):
-                    for plane in range(planes):
-                        nc.tensor.transpose(
-                            turned[:, i, plane, :],
-                            source[:, bank * in_bank + i, plane * P : (plane + 1) * P],
-                            identity[:],
-                        )
-                width = in_bank * P * planes
-                copies[bank](
-                    out=grouped[:, bank * width : (bank + 1) * width].rearrange(
-                        "p (i r u) -> p i r u", i=in_bank, u=planes
-                    ),
-                    in_=turned[:].rearrange("p i u r -> p i r u"),
-                )
+            turned = turned_pool.tile([P, count, planes, P], source.dtype, tag="turned")
+            for i in range(count):
+                for plane in range(planes):
+                    nc.tensor.transpose(
+                        turned[:, i, plane, :], source[:, first + i, plane * P : (plane + 1) * P], identity[:]
+                    )
+            copy_out(
+                out=grouped[:, first * P * planes : (first + count) * P * planes].rearrange(
+                    "p (i r u) -> p i r u", i=count, u=planes
+                ),
+                in_=turned[:].rearrange("p i u r -> p i r u"),
+            )
 
-        def quantise(operand):
+        def quantise(piece):
+            operand, first, count = piece
+            columns = slice(first * P, (first + count) * P)
             nc.vector.quantize_mx(
-                out=operand["codes"][:].bitcast(FP8X4), scales=operand["scales"][:], in_=operand["grouped"][:]
+                out=operand["codes"][:, columns].bitcast(FP8X4),
+                scales=operand["scales"][:, columns],
+                in_=operand["grouped"][:, first * P * PACK : (first + count) * P * PACK],
             )
 
         def mx_pass(acc, stationary, block, moving, start, stop):
@@ -141,18 +148,12 @@ def tile_nodeembeddinglayer_pa_kernel(tc, x, contexts, attn, Wn, bn, Wc, bc, Wu,
                 stop=stop,
             )
 
-        by_scalar = (nc.scalar.copy, nc.scalar.copy)
-        shared = (nc.scalar.copy, nc.vector.tensor_copy)
-
-        ctx_words = words(ctx_raw, CONTEXTS)
         wc_words = words(wc_raw, HALVES * GROUP)
         wn_words = words(wn_raw, HALVES * GROUP)
-        wu_words = words(wu_raw, F_OUT // P)
+        wu_words = words(wu_raw, SIDES * GROUP)
         h_values = [keep.tile([P, K_PASS], BF16, name="h_values%d" % half) for half in range(HALVES)]
 
-        ctx_ops = [
-            new_operand("ctx%d" % g, ctx_words[:, g * GROUP : (g + 1) * GROUP, :]) for g in range(CONTEXTS // GROUP)
-        ]
+        ctx_op = new_operand("ctx", words(ctx_raw, CONTEXTS))
         x_op = new_operand("x", words(x_raw, 1))
         wc_ops = [new_operand("wc%d" % g, wc_words[:, g * GROUP : (g + 1) * GROUP, :]) for g in range(HALVES)]
         wn_ops = [new_operand("wn%d" % g, wn_words[:, g * GROUP : (g + 1) * GROUP, :]) for g in range(HALVES)]
@@ -165,7 +166,7 @@ def tile_nodeembeddinglayer_pa_kernel(tc, x, contexts, attn, Wn, bn, Wc, bc, Wu,
                     "wu%d%d" % (g, side),
                     wu_words[:, side * GROUP : (side + 1) * GROUP, g * K_PASS // 2 : (g + 1) * K_PASS // 2],
                 )
-                for side in range(F_OUT // BANK)
+                for side in range(SIDES)
             ]
             for g in range(HALVES)
         ]
@@ -175,48 +176,50 @@ def tile_nodeembeddinglayer_pa_kernel(tc, x, contexts, attn, Wn, bn, Wc, bc, Wu,
         bias_weights = keep.tile([P, P], BF16, name="bias_weights")
         nc.vector.memset(bias_weights[:], 0.0)
         nc.vector.memset(bias_weights[:, CONTEXTS : CONTEXTS + 1], 1.0)
-
-        turn(wc_ops[0], shared)
-        turn(ctx_ops[0], shared)
-        quantise(wc_ops[0])
-        quantise(ctx_ops[0])
-        turn(ctx_ops[1], by_scalar)
-
         nc.vector.tensor_copy(out=bias_weights[:, 0:CONTEXTS], in_=mean_weights[:])
+
+        waiting = (
+            pairs_of(wc_ops[0]) + pairs_of(ctx_op) + pairs_of(x_op) + pairs_of(wn_ops[0]) + pairs_of(wc_ops[1])
+            + pairs_of(wn_ops[1]) + pairs_of(wu_ops[0][0]) + pairs_of(wu_ops[0][1]) + pairs_of(h_ops[0])
+        )
+        waiting_late = pairs_of(wu_ops[1][0]) + pairs_of(wu_ops[1][1])
+
+        first_pieces, waiting = waiting[:4], waiting[4:]
+        turn(first_pieces[0], nc.scalar.copy)
+        turn(first_pieces[1], nc.vector.tensor_copy)
+        turn(first_pieces[2], nc.scalar.copy)
+        turn(first_pieces[3], nc.scalar.copy)
+        for piece in first_pieces:
+            quantise(piece)
+        turned_last_round, waiting = waiting[:1], waiting[1:]
+        turn(turned_last_round[0], nc.scalar.copy)
+
         bias_turned = turned_pool.tile([P, P], BF16, tag="turned")
         nc.tensor.transpose(bias_turned[:], bias_weights[:], identity_values[:])
         bias_weights_t = keep.tile([P, P], BF16, name="bias_weights_t")
         nc.scalar.copy(out=bias_weights_t[:], in_=bias_turned[:])
 
-        turned_last_round = [ctx_ops[1]]
-        waiting = [
-            ctx_ops[2], ctx_ops[3], x_op, wn_ops[0], wc_ops[1], wn_ops[1],
-            wu_ops[0][0], wu_ops[1][0], h_ops[0], wu_ops[0][1], wu_ops[1][1],
-        ]
         for half in range(HALVES):
-            sums = [keep.tile([P, BANK], F32, name="sum%d_%d" % (half, c)) for c in range(2)]
-            for group in range(CONTEXTS // GROUP):
-                products = []
-                for i in range(GROUP):
-                    product = product_pool.tile([P, BANK], F32, tag="product")
-                    mx_pass(product, ctx_ops[group], i, wc_ops[half], True, True)
-                    products.append(product)
-                for operand in turned_last_round:
-                    quantise(operand)
-                for i in range(GROUP):
-                    k = group * GROUP + i
+            sums = [keep.tile([P, BANK], F32, name="sum%d_%d" % (half, c)) for c in range(PAIR)]
+            for first in range(0, CONTEXTS, PAIR):
+                for c in range(PAIR):
+                    k = first + c
                     weight = mean_weights[:, k : k + 1]
-                    if k < 2:
-                        nc.scalar.activation(out=sums[k][:], in_=products[i][:], func=COPY, scale=weight)
+                    product = product_pool.tile([P, BANK], F32, tag="product")
+                    mx_pass(product, ctx_op, k, wc_ops[half], True, True)
+                    if first == 0:
+                        nc.scalar.activation(out=sums[c][:], in_=product[:], func=COPY, scale=weight)
                     else:
                         nc.vector.scalar_tensor_tensor(
-                            out=sums[k % 2][:], in0=products[i][:], scalar=weight, in1=sums[k % 2][:],
-                            op0=MULT, op1=ADD,
+                            out=sums[c][:], in0=product[:], scalar=weight, in1=sums[c][:], op0=MULT, op1=ADD
                         )
-                turned_last_round = waiting[:PREPARED_PER_ROUND]
-                waiting = waiting[PREPARED_PER_ROUND:]
-                for operand in turned_last_round:
-                    turn(operand, by_scalar)
+                for piece in turned_last_round:
+                    quantise(piece)
+                turned_last_round, waiting = waiting[:PREPARED_PER_ROUND], waiting[PREPARED_PER_ROUND:]
+                spare = PREPARED_PER_ROUND - len(turned_last_round)
+                only_turned, waiting_late = waiting_late[:spare], waiting_late[spare:]
+                for piece in turned_last_round + only_turned:
+                    turn(piece, nc.scalar.copy)
             xt = product_pool.tile([P, BANK], F32, tag="product")
             mx_pass(xt, x_op, 0, wn_ops[half], True, True)
             biases = product_pool.tile([P, BANK], F32, tag="product")
@@ -231,16 +234,19 @@ def tile_nodeembeddinglayer_pa_kernel(tc, x, contexts, attn, Wn, bn, Wc, bc, Wu,
             )
             nc.vector.tensor_add(out=h_values[half][:], in0=sums[0][:], in1=sums[1][:])
 
-        sides = range(F_OUT // BANK)
         out_sums = []
-        for side in sides:
+        for side in range(SIDES):
             out_sum = product_pool.tile([P, BANK], F32, tag="product")
             mx_pass(out_sum, h_ops[0], 0, wu_ops[0][side], True, False)
             out_sums.append(out_sum)
-        turn(h_ops[1], by_scalar)
-        quantise(h_ops[1])
+        last_h = pairs_of(h_ops[1])[0]
+        turn(last_h, nc.scalar.copy)
+        for side in range(SIDES):
+            for piece in pairs_of(wu_ops[1][side]):
+                quantise(piece)
+        quantise(last_h)
         result = keep.tile([P, F_OUT], F32, name="result")
-        for side in sides:
+        for side in range(SIDES):
             columns = slice(side * BANK, (side + 1) * BANK)
             mx_pass(out_sums[side], h_ops[1], 0, wu_ops[1][side], False, True)
             nc.vector.tensor_add(out=result[:, columns], in0=out_sums[side][:], in1=bu_rows[:, columns])

@@ -28,6 +28,7 @@ SIDES = F_OUT // BANK
 GROUP = 4
 PAIR = 2
 PREPARED_PER_ROUND = 2
+GPSIMD_EVERY = 4
 
 FLOPS = 2 * (NODES * F_IN * HIDDEN + NODES * CONTEXTS * F_IN * HIDDEN + NODES * HIDDEN * F_OUT)
 
@@ -39,6 +40,7 @@ def tile_nodeembeddinglayer_pa_kernel(tc, x, contexts, attn, Wn, bn, Wc, bc, Wu,
         keep = stack.enter_context(tc.tile_pool(name="keep", bufs=1))
         turned_pool = stack.enter_context(tc.psum_pool(name="turned_pool", bufs=4))
         product_pool = stack.enter_context(tc.psum_pool(name="product_pool", bufs=4))
+        weighted_pool = stack.enter_context(tc.tile_pool(name="weighted_pool", bufs=3))
 
         attn_raw = keep.tile([P, CONTEXTS], BF16, name="attn_raw")
         nc.scalar.dma_start(out=attn_raw[:], in_=attn)
@@ -200,19 +202,29 @@ def tile_nodeembeddinglayer_pa_kernel(tc, x, contexts, attn, Wn, bn, Wc, bc, Wu,
         nc.scalar.copy(out=bias_weights_t[:], in_=bias_turned[:])
 
         for half in range(HALVES):
-            sums = [keep.tile([P, BANK], F32, name="sum%d_%d" % (half, c)) for c in range(PAIR)]
+            vector_sums = [keep.tile([P, BANK], F32, name="sum%d_%d" % (half, c)) for c in range(2)]
+            gpsimd_sum = keep.tile([P, BANK], F32, name="sum%d_gpsimd" % half)
+            on_vector = 0
             for first in range(0, CONTEXTS, PAIR):
-                for c in range(PAIR):
-                    k = first + c
+                for k in range(first, first + PAIR):
                     weight = mean_weights[:, k : k + 1]
                     product = product_pool.tile([P, BANK], F32, tag="product")
                     mx_pass(product, ctx_op, k, wc_ops[half], True, True)
-                    if first == 0:
-                        nc.scalar.activation(out=sums[c][:], in_=product[:], func=COPY, scale=weight)
+                    if k == GPSIMD_EVERY - 1:
+                        nc.scalar.activation(out=gpsimd_sum[:], in_=product[:], func=COPY, scale=weight)
+                    elif k % GPSIMD_EVERY == GPSIMD_EVERY - 1:
+                        weighted = weighted_pool.tile([P, BANK], F32, tag="weighted")
+                        nc.scalar.activation(out=weighted[:], in_=product[:], func=COPY, scale=weight)
+                        nc.gpsimd.tensor_tensor(out=gpsimd_sum[:], in0=gpsimd_sum[:], in1=weighted[:], op=ADD)
+                    elif on_vector < 2:
+                        nc.scalar.activation(out=vector_sums[on_vector][:], in_=product[:], func=COPY, scale=weight)
+                        on_vector += 1
                     else:
+                        running = vector_sums[on_vector % 2]
                         nc.vector.scalar_tensor_tensor(
-                            out=sums[c][:], in0=product[:], scalar=weight, in1=sums[c][:], op0=MULT, op1=ADD
+                            out=running[:], in0=product[:], scalar=weight, in1=running[:], op0=MULT, op1=ADD
                         )
+                        on_vector += 1
                 for piece in turned_last_round:
                     quantise(piece)
                 turned_last_round, waiting = waiting[:PREPARED_PER_ROUND], waiting[PREPARED_PER_ROUND:]
@@ -227,12 +239,14 @@ def tile_nodeembeddinglayer_pa_kernel(tc, x, contexts, attn, Wn, bn, Wc, bc, Wu,
                 out=biases[:], lhsT=bias_weights_t[:], rhs=bias_rows[:, half * BANK : (half + 1) * BANK],
                 start=True, stop=True,
             )
-            nc.vector.tensor_add(out=sums[0][:], in0=xt[:], in1=sums[0][:])
-            in_h_order = sums[1][:].rearrange("n (u e p) -> n u e p", u=2, e=2)
+            first_sum, second_sum = vector_sums[on_vector % 2], vector_sums[(on_vector + 1) % 2]
+            nc.vector.tensor_add(out=first_sum[:], in0=xt[:], in1=first_sum[:])
+            in_h_order = second_sum[:].rearrange("n (u e p) -> n u e p", u=2, e=2)
             nc.vector.tensor_tensor(
                 out=in_h_order, in0=biases[:].rearrange("n (u p e) -> n u e p", u=2, e=2), in1=in_h_order, op=ADD
             )
-            nc.vector.tensor_add(out=h_values[half][:], in0=sums[0][:], in1=sums[1][:])
+            nc.vector.tensor_add(out=first_sum[:], in0=gpsimd_sum[:], in1=first_sum[:])
+            nc.vector.tensor_add(out=h_values[half][:], in0=first_sum[:], in1=second_sum[:])
 
         out_sums = []
         for side in range(SIDES):

@@ -27,8 +27,7 @@ SIDES = F_OUT // BANK
 
 GROUP = 4
 PAIR = 2
-PREPARED_PER_ROUND = 2
-GPSIMD_EVERY = 4
+PREPARED_PER_ROUND = (2, 1)
 
 FLOPS = 2 * (NODES * F_IN * HIDDEN + NODES * CONTEXTS * F_IN * HIDDEN + NODES * HIDDEN * F_OUT)
 
@@ -40,7 +39,6 @@ def tile_nodeembeddinglayer_pa_kernel(tc, x, contexts, attn, Wn, bn, Wc, bc, Wu,
         keep = stack.enter_context(tc.tile_pool(name="keep", bufs=1))
         turned_pool = stack.enter_context(tc.psum_pool(name="turned_pool", bufs=4))
         product_pool = stack.enter_context(tc.psum_pool(name="product_pool", bufs=4))
-        weighted_pool = stack.enter_context(tc.tile_pool(name="weighted_pool", bufs=3))
 
         attn_raw = keep.tile([P, CONTEXTS], BF16, name="attn_raw")
         nc.scalar.dma_start(out=attn_raw[:], in_=attn)
@@ -92,9 +90,10 @@ def tile_nodeembeddinglayer_pa_kernel(tc, x, contexts, attn, Wn, bn, Wc, bc, Wu,
         identity_values = keep.tile([P, P], BF16, name="identity_values")
         make_identity(nc, identity_values[:])
 
-        def new_operand(name, source):
-            columns = source.shape[1] * P
+        def new_operand(name, blocks, source):
+            columns = blocks * P
             return {
+                "blocks": blocks,
                 "source": source,
                 "grouped": keep.tile([P, columns * PACK], BF16, name=name + "_grouped", align_bytes=64),
                 "codes": keep.tile([P, columns], U32, name=name + "_codes", align_bytes=64),
@@ -102,29 +101,23 @@ def tile_nodeembeddinglayer_pa_kernel(tc, x, contexts, attn, Wn, bn, Wc, bc, Wu,
             }
 
         def pairs_of(operand):
-            blocks = operand["source"].shape[1]
-            step = min(blocks, PAIR)
-            return [(operand, first, step) for first in range(0, blocks, step)]
+            step = min(operand["blocks"], PAIR)
+            return [(operand, first, step) for first in range(0, operand["blocks"], step)]
 
         def words(raw, blocks):
             return raw[:].bitcast(F32).rearrange("p (b w) -> p b w", b=blocks)
 
         def turn(piece, copy_out):
             operand, first, count = piece
-            source = operand["source"]
-            as_words = source.dtype == F32
-            identity = identity_words if as_words else identity_values
-            grouped = operand["grouped"][:].bitcast(F32) if as_words else operand["grouped"][:]
-            planes = source.shape[2] // P
-            turned = turned_pool.tile([P, count, planes, P], source.dtype, tag="turned")
+            turned = turned_pool.tile([P, count, 2, P], F32, tag="turned")
             for i in range(count):
-                for plane in range(planes):
+                for u in range(2):
                     nc.tensor.transpose(
-                        turned[:, i, plane, :], source[:, first + i, plane * P : (plane + 1) * P], identity[:]
+                        turned[:, i, u, :], operand["source"][:, first + i, u * P : (u + 1) * P], identity_words[:]
                     )
             copy_out(
-                out=grouped[:, first * P * planes : (first + count) * P * planes].rearrange(
-                    "p (i r u) -> p i r u", i=count, u=planes
+                out=operand["grouped"][:].bitcast(F32)[:, first * P * 2 : (first + count) * P * 2].rearrange(
+                    "p (i r u) -> p i r u", i=count, u=2
                 ),
                 in_=turned[:].rearrange("p i u r -> p i r u"),
             )
@@ -153,19 +146,17 @@ def tile_nodeembeddinglayer_pa_kernel(tc, x, contexts, attn, Wn, bn, Wc, bc, Wu,
         wc_words = words(wc_raw, HALVES * GROUP)
         wn_words = words(wn_raw, HALVES * GROUP)
         wu_words = words(wu_raw, SIDES * GROUP)
-        h_values = [keep.tile([P, K_PASS], BF16, name="h_values%d" % half) for half in range(HALVES)]
 
-        ctx_op = new_operand("ctx", words(ctx_raw, CONTEXTS))
-        x_op = new_operand("x", words(x_raw, 1))
-        wc_ops = [new_operand("wc%d" % g, wc_words[:, g * GROUP : (g + 1) * GROUP, :]) for g in range(HALVES)]
-        wn_ops = [new_operand("wn%d" % g, wn_words[:, g * GROUP : (g + 1) * GROUP, :]) for g in range(HALVES)]
-        h_ops = [
-            new_operand("h%d" % g, h_values[g][:].rearrange("p (b v) -> p b v", b=1)) for g in range(HALVES)
-        ]
+        ctx_op = new_operand("ctx", CONTEXTS, words(ctx_raw, CONTEXTS))
+        x_op = new_operand("x", 1, words(x_raw, 1))
+        wc_ops = [new_operand("wc%d" % g, GROUP, wc_words[:, g * GROUP : (g + 1) * GROUP, :]) for g in range(HALVES)]
+        wn_ops = [new_operand("wn%d" % g, GROUP, wn_words[:, g * GROUP : (g + 1) * GROUP, :]) for g in range(HALVES)]
+        h_ops = [new_operand("h%d" % g, 1, None) for g in range(HALVES)]
         wu_ops = [
             [
                 new_operand(
                     "wu%d%d" % (g, side),
+                    GROUP,
                     wu_words[:, side * GROUP : (side + 1) * GROUP, g * K_PASS // 2 : (g + 1) * K_PASS // 2],
                 )
                 for side in range(SIDES)
@@ -182,7 +173,7 @@ def tile_nodeembeddinglayer_pa_kernel(tc, x, contexts, attn, Wn, bn, Wc, bc, Wu,
 
         waiting = (
             pairs_of(wc_ops[0]) + pairs_of(ctx_op) + pairs_of(x_op) + pairs_of(wn_ops[0]) + pairs_of(wc_ops[1])
-            + pairs_of(wn_ops[1]) + pairs_of(wu_ops[0][0]) + pairs_of(wu_ops[0][1]) + pairs_of(h_ops[0])
+            + pairs_of(wn_ops[1]) + pairs_of(wu_ops[0][0]) + pairs_of(wu_ops[0][1])
         )
         waiting_late = pairs_of(wu_ops[1][0]) + pairs_of(wu_ops[1][1])
 
@@ -195,70 +186,67 @@ def tile_nodeembeddinglayer_pa_kernel(tc, x, contexts, attn, Wn, bn, Wc, bc, Wu,
             quantise(piece)
         turned_last_round, waiting = waiting[:1], waiting[1:]
         turn(turned_last_round[0], nc.scalar.copy)
-
         bias_turned = turned_pool.tile([P, P], BF16, tag="turned")
         nc.tensor.transpose(bias_turned[:], bias_weights[:], identity_values[:])
         bias_weights_t = keep.tile([P, P], BF16, name="bias_weights_t")
         nc.scalar.copy(out=bias_weights_t[:], in_=bias_turned[:])
 
+        sums = [[keep.tile([P, BANK], F32, name="sum%d_%d" % (half, c)) for c in range(2)] for half in range(HALVES)]
+        rounds = 0
         for half in range(HALVES):
-            vector_sums = [keep.tile([P, BANK], F32, name="sum%d_%d" % (half, c)) for c in range(2)]
-            gpsimd_sum = keep.tile([P, BANK], F32, name="sum%d_gpsimd" % half)
-            on_vector = 0
-            for first in range(0, CONTEXTS, PAIR):
-                for k in range(first, first + PAIR):
-                    weight = mean_weights[:, k : k + 1]
+            terms = [(ctx_op, k, wc_ops[half], mean_weights[:, k : k + 1]) for k in range(CONTEXTS)]
+            terms.append((x_op, 0, wn_ops[half], 1.0))
+            for first in range(0, len(terms), PAIR):
+                for index in range(first, min(first + PAIR, len(terms))):
+                    stationary, block, moving, weight = terms[index]
+                    running = sums[half][index % 2]
                     product = product_pool.tile([P, BANK], F32, tag="product")
-                    mx_pass(product, ctx_op, k, wc_ops[half], True, True)
-                    if k == GPSIMD_EVERY - 1:
-                        nc.scalar.activation(out=gpsimd_sum[:], in_=product[:], func=COPY, scale=weight)
-                    elif k % GPSIMD_EVERY == GPSIMD_EVERY - 1:
-                        weighted = weighted_pool.tile([P, BANK], F32, tag="weighted")
-                        nc.scalar.activation(out=weighted[:], in_=product[:], func=COPY, scale=weight)
-                        nc.gpsimd.tensor_tensor(out=gpsimd_sum[:], in0=gpsimd_sum[:], in1=weighted[:], op=ADD)
-                    elif on_vector < 2:
-                        nc.scalar.activation(out=vector_sums[on_vector][:], in_=product[:], func=COPY, scale=weight)
-                        on_vector += 1
+                    mx_pass(product, stationary, block, moving, True, True)
+                    if index < 2:
+                        nc.scalar.activation(out=running[:], in_=product[:], func=COPY, scale=weight)
                     else:
-                        running = vector_sums[on_vector % 2]
                         nc.vector.scalar_tensor_tensor(
                             out=running[:], in0=product[:], scalar=weight, in1=running[:], op0=MULT, op1=ADD
                         )
-                        on_vector += 1
                 for piece in turned_last_round:
                     quantise(piece)
-                turned_last_round, waiting = waiting[:PREPARED_PER_ROUND], waiting[PREPARED_PER_ROUND:]
-                spare = PREPARED_PER_ROUND - len(turned_last_round)
+                prepared = PREPARED_PER_ROUND[rounds % 2]
+                rounds += 1
+                turned_last_round, waiting = waiting[:prepared], waiting[prepared:]
+                spare = prepared - len(turned_last_round)
                 only_turned, waiting_late = waiting_late[:spare], waiting_late[spare:]
                 for piece in turned_last_round + only_turned:
                     turn(piece, nc.scalar.copy)
-            xt = product_pool.tile([P, BANK], F32, tag="product")
-            mx_pass(xt, x_op, 0, wn_ops[half], True, True)
-            biases = product_pool.tile([P, BANK], F32, tag="product")
-            nc.tensor.matmul(
-                out=biases[:], lhsT=bias_weights_t[:], rhs=bias_rows[:, half * BANK : (half + 1) * BANK],
-                start=True, stop=True,
-            )
-            first_sum, second_sum = vector_sums[on_vector % 2], vector_sums[(on_vector + 1) % 2]
-            nc.vector.tensor_add(out=first_sum[:], in0=xt[:], in1=first_sum[:])
-            in_h_order = second_sum[:].rearrange("n (u e p) -> n u e p", u=2, e=2)
-            nc.vector.tensor_tensor(
-                out=in_h_order, in0=biases[:].rearrange("n (u p e) -> n u e p", u=2, e=2), in1=in_h_order, op=ADD
-            )
-            nc.vector.tensor_add(out=first_sum[:], in0=gpsimd_sum[:], in1=first_sum[:])
-            nc.vector.tensor_add(out=h_values[half][:], in0=first_sum[:], in1=second_sum[:])
 
+        bias_columns = bias_rows[:].rearrange("r (b p e) -> r b e p", b=HALVES * 2, e=2)
+        for half in range(HALVES):
+            h_turned = turned_pool.tile([P, PACK, P], F32, tag="turned")
+            for t in range(PACK):
+                nc.tensor.matmul(
+                    out=h_turned[:, t, :], lhsT=bias_columns[:, half * 2 + t // 2, t % 2, :], rhs=bias_weights_t[:],
+                    start=(t == 0), stop=False,
+                )
+            for c in (1, 0):
+                for t in range(PACK):
+                    nc.tensor.matmul(
+                        out=h_turned[:, t, :], lhsT=sums[half][c][:, t * P : (t + 1) * P], rhs=identity_words[:],
+                        is_transpose=True, start=False, stop=(c == 0 and t == PACK - 1),
+                    )
+            nc.scalar.copy(
+                out=h_ops[half]["grouped"][:].rearrange("p (r t) -> p r t", t=PACK),
+                in_=h_turned[:].rearrange("p t r -> p r t"),
+            )
+
+        quantise(pairs_of(h_ops[0])[0])
         out_sums = []
         for side in range(SIDES):
             out_sum = product_pool.tile([P, BANK], F32, tag="product")
             mx_pass(out_sum, h_ops[0], 0, wu_ops[0][side], True, False)
             out_sums.append(out_sum)
-        last_h = pairs_of(h_ops[1])[0]
-        turn(last_h, nc.scalar.copy)
         for side in range(SIDES):
             for piece in pairs_of(wu_ops[1][side]):
                 quantise(piece)
-        quantise(last_h)
+        quantise(pairs_of(h_ops[1])[0])
         result = keep.tile([P, F_OUT], F32, name="result")
         for side in range(SIDES):
             columns = slice(side * BANK, (side + 1) * BANK)

@@ -28,6 +28,7 @@ SIDES = F_OUT // BANK
 GROUP = 4
 PAIR = 2
 PREPARED_PER_ROUND = (2, 1)
+SCALAR_EVERY = 6
 
 FLOPS = 2 * (NODES * F_IN * HIDDEN + NODES * CONTEXTS * F_IN * HIDDEN + NODES * HIDDEN * F_OUT)
 
@@ -191,23 +192,32 @@ def tile_nodeembeddinglayer_pa_kernel(tc, x, contexts, attn, Wn, bn, Wc, bc, Wu,
         bias_weights_t = keep.tile([P, P], BF16, name="bias_weights_t")
         nc.scalar.copy(out=bias_weights_t[:], in_=bias_turned[:])
 
-        sums = [[keep.tile([P, BANK], F32, name="sum%d_%d" % (half, c)) for c in range(2)] for half in range(HALVES)]
+        parts = []
         rounds = 0
         for half in range(HALVES):
             terms = [(ctx_op, k, wc_ops[half], mean_weights[:, k : k + 1]) for k in range(CONTEXTS)]
             terms.append((x_op, 0, wn_ops[half], 1.0))
+            sums = [keep.tile([P, BANK], F32, name="sum%d_%d" % (half, c)) for c in range(2)]
+            in_sums = 0
+            alone = []
             for first in range(0, len(terms), PAIR):
                 for index in range(first, min(first + PAIR, len(terms))):
                     stationary, block, moving, weight = terms[index]
-                    running = sums[half][index % 2]
                     product = product_pool.tile([P, BANK], F32, tag="product")
                     mx_pass(product, stationary, block, moving, True, True)
-                    if index < 2:
-                        nc.scalar.activation(out=running[:], in_=product[:], func=COPY, scale=weight)
+                    if index % SCALAR_EVERY == SCALAR_EVERY - 1:
+                        weighted = keep.tile([P, BANK], F32, name="weighted%d_%d" % (half, index))
+                        nc.scalar.activation(out=weighted[:], in_=product[:], func=COPY, scale=weight)
+                        alone.append(weighted)
+                    elif in_sums < 2:
+                        nc.scalar.activation(out=sums[in_sums][:], in_=product[:], func=COPY, scale=weight)
+                        in_sums += 1
                     else:
+                        running = sums[in_sums % 2]
                         nc.vector.scalar_tensor_tensor(
                             out=running[:], in0=product[:], scalar=weight, in1=running[:], op0=MULT, op1=ADD
                         )
+                        in_sums += 1
                 for piece in turned_last_round:
                     quantise(piece)
                 prepared = PREPARED_PER_ROUND[rounds % 2]
@@ -217,6 +227,7 @@ def tile_nodeembeddinglayer_pa_kernel(tc, x, contexts, attn, Wn, bn, Wc, bc, Wu,
                 only_turned, waiting_late = waiting_late[:spare], waiting_late[spare:]
                 for piece in turned_last_round + only_turned:
                     turn(piece, nc.scalar.copy)
+            parts.append(alone + [sums[in_sums % 2], sums[(in_sums - 1) % 2]])
 
         bias_columns = bias_rows[:].rearrange("r (b p e) -> r b e p", b=HALVES * 2, e=2)
         for half in range(HALVES):
@@ -226,11 +237,11 @@ def tile_nodeembeddinglayer_pa_kernel(tc, x, contexts, attn, Wn, bn, Wc, bc, Wu,
                     out=h_turned[:, t, :], lhsT=bias_columns[:, half * 2 + t // 2, t % 2, :], rhs=bias_weights_t[:],
                     start=(t == 0), stop=False,
                 )
-            for c in (1, 0):
+            for part in parts[half]:
                 for t in range(PACK):
                     nc.tensor.matmul(
-                        out=h_turned[:, t, :], lhsT=sums[half][c][:, t * P : (t + 1) * P], rhs=identity_words[:],
-                        is_transpose=True, start=False, stop=(c == 0 and t == PACK - 1),
+                        out=h_turned[:, t, :], lhsT=part[:, t * P : (t + 1) * P], rhs=identity_words[:],
+                        is_transpose=True, start=False, stop=(part is parts[half][-1] and t == PACK - 1),
                     )
             nc.scalar.copy(
                 out=h_ops[half]["grouped"][:].rearrange("p (r t) -> p r t", t=PACK),

@@ -36,7 +36,6 @@ FLOPS = 2 * (NODES * F_IN * HIDDEN + NODES * CONTEXTS * F_IN * HIDDEN + NODES * 
 def tile_nodeembeddinglayer_pa_kernel(tc, x, contexts, attn, Wn, bn, Wc, bc, Wu, bu, out):
     nc = tc.nc
     with ExitStack() as stack:
-        stack.enter_context(tc.manual_schedule())
         keep = stack.enter_context(tc.tile_pool(name="keep", bufs=1))
         turned_pool = stack.enter_context(tc.psum_pool(name="turned_pool", bufs=4))
         product_pool = stack.enter_context(tc.psum_pool(name="product_pool", bufs=4))

@@ -36,16 +36,15 @@ FLOPS = 2 * (NODES * F_IN * HIDDEN + NODES * CONTEXTS * F_IN * HIDDEN + NODES * 
 def tile_nodeembeddinglayer_pa_kernel(tc, x, contexts, attn, Wn, bn, Wc, bc, Wu, bu, out):
     nc = tc.nc
     with ExitStack() as stack:
+        stack.enter_context(tc.manual_schedule())
         keep = stack.enter_context(tc.tile_pool(name="keep", bufs=1))
         turned_pool = stack.enter_context(tc.psum_pool(name="turned_pool", bufs=4))
         product_pool = stack.enter_context(tc.psum_pool(name="product_pool", bufs=4))
 
         attn_raw = keep.tile([P, CONTEXTS], BF16, name="attn_raw")
-        nc.scalar.dma_start(out=attn_raw[:], in_=attn)
+        nc.sync.dma_start(out=attn_raw[:], in_=attn)
         bias_rows = keep.tile([P, HIDDEN], BF16, name="bias_rows")
         nc.vector.memset(bias_rows[:], 0.0)
-        nc.scalar.dma_start(out=bias_rows[0:CONTEXTS, :], in_=bc.partition_broadcast(CONTEXTS))
-        nc.scalar.dma_start(out=bias_rows[CONTEXTS : CONTEXTS + 1, :], in_=bn.unsqueeze(0))
 
         wc_raw = keep.tile([P, HALVES * GROUP * F_IN], BF16, name="wc_raw")
         wn_raw = keep.tile([P, HALVES * GROUP * F_IN], BF16, name="wn_raw")
@@ -83,6 +82,8 @@ def tile_nodeembeddinglayer_pa_kernel(tc, x, contexts, attn, Wn, bn, Wc, bc, Wu,
         load_hidden_rows(wn_raw, Wn, 1)
         for pair in range(SIDES * GROUP // PAIR):
             load_output_rows(pair)
+        nc.sync.dma_start(out=bias_rows[0:CONTEXTS, :], in_=bc.partition_broadcast(CONTEXTS))
+        nc.sync.dma_start(out=bias_rows[CONTEXTS : CONTEXTS + 1, :], in_=bn.unsqueeze(0))
         nc.sync.dma_start(out=bu_rows[:], in_=bu.partition_broadcast(P))
 
         identity_words = keep.tile([P, P], F32, name="identity_words")

from contextlib import ExitStack

import concourse.mybir as mybir
from concourse.masks import make_identity

F32 = mybir.dt.float32
BF16 = mybir.dt.bfloat16
U32 = mybir.dt.uint32
U8 = mybir.dt.uint8
FP8X4 = mybir.dt.float8_e4m3fn_x4
MULT = mybir.AluOpType.mult
ADD = mybir.AluOpType.add
COPY = mybir.ActivationFunctionType.Copy

P = 128
PACK = 4
K_PASS = P * PACK
BANK = 512

NODES = 128
CONTEXTS = 16
F_IN = 512
HIDDEN = 1024
F_OUT = 1024
HALVES = HIDDEN // K_PASS
SIDES = F_OUT // BANK

GROUP = 4
PAIR = 2
PREPARED_PER_ROUND = (2, 1)
SCALAR_EVERY = 6

FLOPS = 2 * (NODES * F_IN * HIDDEN + NODES * CONTEXTS * F_IN * HIDDEN + NODES * HIDDEN * F_OUT)


def tile_nodeembeddinglayer_pa_kernel(tc, x, contexts, attn, Wn, bn, Wc, bc, Wu, bu, out):
    nc = tc.nc
    with ExitStack() as stack:
        stack.enter_context(tc.manual_schedule())
        keep = stack.enter_context(tc.tile_pool(name="keep", bufs=1))
        turned_pool = stack.enter_context(tc.psum_pool(name="turned_pool", bufs=4))
        product_pool = stack.enter_context(tc.psum_pool(name="product_pool", bufs=4))

        attn_raw = keep.tile([P, CONTEXTS], BF16, name="attn_raw")
        nc.sync.dma_start(out=attn_raw[:], in_=attn)
        bias_rows = keep.tile([P, HIDDEN], BF16, name="bias_rows")
        nc.vector.memset(bias_rows[:], 0.0)

        wc_raw = keep.tile([P, HALVES * GROUP * F_IN], BF16, name="wc_raw")
        wn_raw = keep.tile([P, HALVES * GROUP * F_IN], BF16, name="wn_raw")
        ctx_raw = keep.tile([P, CONTEXTS * F_IN], BF16, name="ctx_raw")
        x_raw = keep.tile([P, F_IN], BF16, name="x_raw")
        wu_raw = keep.tile([P, SIDES * GROUP * HIDDEN], BF16, name="wu_raw")
        bu_rows = keep.tile([P, F_OUT], BF16, name="bu_rows")

        def load_hidden_rows(raw, weight, half):
            for u in range(2):
                pair = half * 2 + u
                nc.sync.dma_start(
                    out=raw[:, pair * PAIR * F_IN : (pair + 1) * PAIR * F_IN],
                    in_=weight.rearrange("(g p e) f -> g p (e f)", g=HALVES * 2, p=P, e=PAIR)[pair],
                )

        def load_contexts(pair):
            columns = slice(pair * PAIR * F_IN, (pair + 1) * PAIR * F_IN)
            nc.sync.dma_start(out=ctx_raw[:, columns], in_=contexts.rearrange("n k f -> n (k f)")[:, columns])

        def load_output_rows(pair):
            nc.sync.dma_start(
                out=wu_raw[:, pair * PAIR * HIDDEN : (pair + 1) * PAIR * HIDDEN].rearrange(
                    "p (b h) -> p b h", b=PAIR
                ),
                in_=Wu.rearrange("(b p) h -> p b h", p=P)[:, pair * PAIR : (pair + 1) * PAIR, :],
            )

        load_hidden_rows(wc_raw, Wc, 0)
        for pair in range(CONTEXTS // PAIR):
            load_contexts(pair)
        nc.sync.dma_start(out=x_raw[:], in_=x)
        load_hidden_rows(wn_raw, Wn, 0)
        load_hidden_rows(wc_raw, Wc, 1)
        load_hidden_rows(wn_raw, Wn, 1)
        for pair in range(SIDES * GROUP // PAIR):
            load_output_rows(pair)
        nc.sync.dma_start(out=bias_rows[0:CONTEXTS, :], in_=bc.partition_broadcast(CONTEXTS))
        nc.sync.dma_start(out=bias_rows[CONTEXTS : CONTEXTS + 1, :], in_=bn.unsqueeze(0))
        nc.sync.dma_start(out=bu_rows[:], in_=bu.partition_broadcast(P))

        identity_words = keep.tile([P, P], F32, name="identity_words")
        make_identity(nc, identity_words[:])
        identity_values = keep.tile([P, P], BF16, name="identity_values")
        make_identity(nc, identity_values[:])

        def new_operand(name, blocks, source):
            columns = blocks * P
            return {
                "blocks": blocks,
                "source": source,
                "grouped": keep.tile([P, columns * PACK], BF16, name=name + "_grouped", align_bytes=64),
                "codes": keep.tile([P, columns], U32, name=name + "_codes", align_bytes=64),
                "scales": keep.tile([P, columns], U8, name=name + "_scales", align_bytes=64),
            }

        def pairs_of(operand):
            step = min(operand["blocks"], PAIR)
            return [(operand, first, step) for first in range(0, operand["blocks"], step)]

        def words(raw, blocks):
            return raw[:].bitcast(F32).rearrange("p (b w) -> p b w", b=blocks)

        def turn(piece, copy_out):
            operand, first, count = piece
            turned = turned_pool.tile([P, count, 2, P], F32, tag="turned")
            for i in range(count):
                for u in range(2):
                    nc.tensor.transpose(
                        turned[:, i, u, :], operand["source"][:, first + i, u * P : (u + 1) * P], identity_words[:]
                    )
            copy_out(
                out=operand["grouped"][:].bitcast(F32)[:, first * P * 2 : (first + count) * P * 2].rearrange(
                    "p (i r u) -> p i r u", i=count, u=2
                ),
                in_=turned[:].rearrange("p i u r -> p i r u"),
            )

        def quantise(piece):
            operand, first, count = piece
            columns = slice(first * P, (first + count) * P)
            nc.vector.quantize_mx(
                out=operand["codes"][:, columns].bitcast(FP8X4),
                scales=operand["scales"][:, columns],
                in_=operand["grouped"][:, first * P * PACK : (first + count) * P * PACK],
            )

        def mx_pass(acc, stationary, block, moving, start, stop):
            columns = slice(block * P, (block + 1) * P)
            nc.tensor.matmul_mx(
                out=acc[:],
                lhsT=stationary["codes"][:, columns].bitcast(FP8X4),
                lhsT_scale=stationary["scales"][:, columns],
                rhs=moving["codes"][:].bitcast(FP8X4),
                rhs_scale=moving["scales"][:],
                start=start,
                stop=stop,
            )

        wc_words = words(wc_raw, HALVES * GROUP)
        wn_words = words(wn_raw, HALVES * GROUP)
        wu_words = words(wu_raw, SIDES * GROUP)

        ctx_op = new_operand("ctx", CONTEXTS, words(ctx_raw, CONTEXTS))
        x_op = new_operand("x", 1, words(x_raw, 1))
        wc_ops = [new_operand("wc%d" % g, GROUP, wc_words[:, g * GROUP : (g + 1) * GROUP, :]) for g in range(HALVES)]
        wn_ops = [new_operand("wn%d" % g, GROUP, wn_words[:, g * GROUP : (g + 1) * GROUP, :]) for g in range(HALVES)]
        h_ops = [new_operand("h%d" % g, 1, None) for g in range(HALVES)]
        wu_ops = [
            [
                new_operand(
                    "wu%d%d" % (g, side),
                    GROUP,
                    wu_words[:, side * GROUP : (side + 1) * GROUP, g * K_PASS // 2 : (g + 1) * K_PASS // 2],
                )
                for side in range(SIDES)
            ]
            for g in range(HALVES)
        ]

        mean_weights = keep.tile([P, CONTEXTS], F32, name="mean_weights")
        nc.scalar.activation(out=mean_weights[:], in_=attn_raw[:], func=COPY, scale=1.0 / CONTEXTS)
        bias_weights = keep.tile([P, P], BF16, name="bias_weights")
        nc.vector.memset(bias_weights[:], 0.0)
        nc.vector.memset(bias_weights[:, CONTEXTS : CONTEXTS + 1], 1.0)
        nc.vector.tensor_copy(out=bias_weights[:, 0:CONTEXTS], in_=mean_weights[:])

        waiting = (
            pairs_of(wc_ops[0]) + pairs_of(ctx_op) + pairs_of(x_op) + pairs_of(wn_ops[0]) + pairs_of(wc_ops[1])
            + pairs_of(wn_ops[1]) + pairs_of(wu_ops[0][0]) + pairs_of(wu_ops[0][1])
        )
        waiting_late = pairs_of(wu_ops[1][0]) + pairs_of(wu_ops[1][1])

        first_pieces, waiting = waiting[:4], waiting[4:]
        turn(first_pieces[0], nc.scalar.copy)
        turn(first_pieces[1], nc.vector.tensor_copy)
        turn(first_pieces[2], nc.scalar.copy)
        turn(first_pieces[3], nc.scalar.copy)
        for piece in first_pieces:
            quantise(piece)
        turned_last_round, waiting = waiting[:1], waiting[1:]
        turn(turned_last_round[0], nc.scalar.copy)
        bias_turned = turned_pool.tile([P, P], BF16, tag="turned")
        nc.tensor.transpose(bias_turned[:], bias_weights[:], identity_values[:])
        bias_weights_t = keep.tile([P, P], BF16, name="bias_weights_t")
        nc.scalar.copy(out=bias_weights_t[:], in_=bias_turned[:])

        parts = []
        rounds = 0
        for half in range(HALVES):
            terms = [(ctx_op, k, wc_ops[half], mean_weights[:, k : k + 1]) for k in range(CONTEXTS)]
            terms.append((x_op, 0, wn_ops[half], 1.0))
            sums = [keep.tile([P, BANK], F32, name="sum%d_%d" % (half, c)) for c in range(2)]
            in_sums = 0
            alone = []
            for first in range(0, len(terms), PAIR):
                for index in range(first, min(first + PAIR, len(terms))):
                    stationary, block, moving, weight = terms[index]
                    product = product_pool.tile([P, BANK], F32, tag="product")
                    mx_pass(product, stationary, block, moving, True, True)
                    if index % SCALAR_EVERY == SCALAR_EVERY - 1:
                        weighted = keep.tile([P, BANK], F32, name="weighted%d_%d" % (half, index))
                        nc.scalar.activation(out=weighted[:], in_=product[:], func=COPY, scale=weight)
                        alone.append(weighted)
                    elif in_sums < 2:
                        nc.scalar.activation(out=sums[in_sums][:], in_=product[:], func=COPY, scale=weight)
                        in_sums += 1
                    else:
                        running = sums[in_sums % 2]
                        nc.vector.scalar_tensor_tensor(
                            out=running[:], in0=product[:], scalar=weight, in1=running[:], op0=MULT, op1=ADD
                        )
                        in_sums += 1
                for piece in turned_last_round:
                    quantise(piece)
                prepared = PREPARED_PER_ROUND[rounds % 2]
                rounds += 1
                turned_last_round, waiting = waiting[:prepared], waiting[prepared:]
                spare = prepared - len(turned_last_round)
                only_turned, waiting_late = waiting_late[:spare], waiting_late[spare:]
                for piece in turned_last_round + only_turned:
                    turn(piece, nc.scalar.copy)
            parts.append(alone + [sums[in_sums % 2], sums[(in_sums - 1) % 2]])

        bias_columns = bias_rows[:].rearrange("r (b p e) -> r b e p", b=HALVES * 2, e=2)
        for half in range(HALVES):
            h_turned = turned_pool.tile([P, PACK, P], F32, tag="turned")
            for t in range(PACK):
                nc.tensor.matmul(
                    out=h_turned[:, t, :], lhsT=bias_columns[:, half * 2 + t // 2, t % 2, :], rhs=bias_weights_t[:],
                    start=(t == 0), stop=False,
                )
            for part in parts[half]:
                for t in range(PACK):
                    nc.tensor.matmul(
                        out=h_turned[:, t, :], lhsT=part[:, t * P : (t + 1) * P], rhs=identity_words[:],
                        is_transpose=True, start=False, stop=(part is parts[half][-1] and t == PACK - 1),
                    )
            nc.scalar.copy(
                out=h_ops[half]["grouped"][:].rearrange("p (r t) -> p r t", t=PACK),
                in_=h_turned[:].rearrange("p t r -> p r t"),
            )

        quantise(pairs_of(h_ops[0])[0])
        out_sums = []
        for side in range(SIDES):
            out_sum = product_pool.tile([P, BANK], F32, tag="product")
            mx_pass(out_sum, h_ops[0], 0, wu_ops[0][side], True, False)
            out_sums.append(out_sum)
        for side in range(SIDES):
            for piece in pairs_of(wu_ops[1][side]):
                quantise(piece)
        quantise(pairs_of(h_ops[1])[0])
        result = keep.tile([P, F_OUT], F32, name="result")
        for side in range(SIDES):
            columns = slice(side * BANK, (side + 1) * BANK)
            mx_pass(out_sums[side], h_ops[1], 0, wu_ops[1][side], False, True)
            nc.vector.tensor_add(out=result[:, columns], in0=out_sums[side][:], in1=bu_rows[:, columns])
            nc.sync.dma_start(out=out[:, columns], in_=result[:, columns])
